import numpy as np
import ml_dtypes


BF16 = ml_dtypes.bfloat16


def bf(x):
    return np.asarray(x, np.float32).astype(BF16)


def f64(x):
    return np.asarray(x).astype(np.float64)


E2M1 = np.array([0.0, 0.5, 1.0, 1.5, 2.0, 3.0, 4.0, 6.0, -0.0, -0.5, -1.0, -1.5, -2.0, -3.0, -4.0, -6.0])


def pack_weight(w, fmt):
    k, n = w.shape
    w = f64(bf(w)).reshape(k // 32, 32, n)
    amax = np.abs(w).max(1)
    if fmt == "e4m3":
        byte = np.frexp(amax)[1] - 1 + 127 - 7
    else:
        mant, ex = np.frexp(amax / 6.0)
        byte = np.where(mant > 0.5, ex, ex - 1) + 127
    byte = np.clip(np.where(amax > 0, byte, 1), 1, 254)
    scaled = (w * np.exp2(127.0 - byte)[:, None, :]).reshape(k, n).astype(np.float32)
    by_word = np.ascontiguousarray(scaled.reshape(k // 512, 128, 4, n).transpose(0, 1, 3, 2))
    if fmt == "e4m3":
        words = by_word.astype(ml_dtypes.float8_e4m3fn).view(np.uint8)
    else:
        c = by_word.astype(ml_dtypes.float4_e2m1fn).view(np.uint8) & 0xF
        words = c[..., 0::2] | (c[..., 1::2] << 4)
    return np.ascontiguousarray(words), np.ascontiguousarray(byte.astype(np.uint8).reshape(k // 512, 16, n))


def unpack_weight(words, scales, fmt):
    g, p, n, _ = words.shape
    if fmt == "e4m3":
        vals = np.ascontiguousarray(words).view(ml_dtypes.float8_e4m3fn).astype(np.float64)
    else:
        nib = np.empty((g, p, n, 4), np.uint8)
        nib[..., 0::2] = words & 0xF
        nib[..., 1::2] = words >> 4
        vals = E2M1[nib]
    vals = vals * np.repeat(np.exp2(scales.astype(np.float64) - 127.0), 8, axis=1)[..., None]
    return vals.transpose(0, 1, 3, 2).reshape(g * 512, n)

def pack4(w):
    words, scales = pack_weight(w, "e2m1")
    return words.reshape(words.shape[0], 128, -1), scales


def unpack4(words, scales):
    return unpack_weight(words.reshape(words.shape[0], 128, -1, 2), scales, "e2m1")


def kspread(k):
    return np.exp2(np.repeat(np.random.randint(-6, 7, k // 32), 32).astype(np.float64))


B, T, E, H, HKV, DH, WINDOW = 4, 1024, 2048, 8, 4, 128, 512
ROPE_THETA = 10000.0
EPS = 1e-6


def rms_norm(u, w):
    return u * (1.0 / np.sqrt(np.mean(u * u, axis=-1, keepdims=True) + EPS)) * (1.0 + w)


def rotate_half(u):
    return np.concatenate((-u[..., DH // 2:], u[..., :DH // 2]), axis=-1)


def setup_inputs():
    s = kspread(E)
    x = np.random.standard_normal((B, T, E)) * s
    x_words, x_scales = pack4(x.reshape(B * T, E).T)
    wq_words, wq_scales = pack4((np.random.standard_normal((H * DH, E)) / np.sqrt(E) / s).T)
    wk_words, wk_scales = pack4((np.random.standard_normal((HKV * DH, E)) / np.sqrt(E) / s).T)
    wv_words, wv_scales = pack4((np.random.standard_normal((HKV * DH, E)) * 2.0 / np.sqrt(E) / s).T)
    q_norm_w = bf(np.random.standard_normal(DH) * 0.1)
    k_norm_w = bf(np.random.standard_normal(DH) * 0.1)
    return {"x_words": x_words, "x_scales": x_scales,
            "wq_words": wq_words, "wq_scales": wq_scales,
            "wk_words": wk_words, "wk_scales": wk_scales,
            "wv_words": wv_words, "wv_scales": wv_scales,
            "q_norm_w": q_norm_w,
            "k_norm_w": k_norm_w}


def reference(x_words, x_scales, wq_words, wq_scales, wk_words, wk_scales, wv_words, wv_scales, q_norm_w, k_norm_w):
    xq = unpack4(x_words, x_scales).T.reshape(B, T, E)
    q = (xq @ unpack4(wq_words, wq_scales)).reshape(B, T, H, DH).transpose(0, 2, 1, 3)
    k = (xq @ unpack4(wk_words, wk_scales)).reshape(B, T, HKV, DH).transpose(0, 2, 1, 3)
    v = (xq @ unpack4(wv_words, wv_scales)).reshape(B, T, HKV, DH).transpose(0, 2, 1, 3)
    q = rms_norm(q, f64(q_norm_w))
    k = rms_norm(k, f64(k_norm_w))
    pos = f64(np.arange(T))
    inv_freq = 1.0 / (ROPE_THETA ** (f64(np.arange(0, DH, 2)) / DH))
    freqs = pos[:, None] * inv_freq[None, :]
    emb = np.concatenate((freqs, freqs), axis=-1)
    cos = np.cos(emb)[None, None, :, :]
    sin = np.sin(emb)[None, None, :, :]
    q = q * cos + rotate_half(q) * sin
    k = k * cos + rotate_half(k) * sin
    q = q * (DH ** -0.5)
    return q, k, v

@@ -1,0 +1,342 @@
+from contextlib import ExitStack
+import math
+
+import concourse.mybir as mybir
+
+F32 = mybir.dt.float32
+BF16 = mybir.dt.bfloat16
+I32 = mybir.dt.int32
+U8 = mybir.dt.uint8
+FP4X4 = mybir.dt.float4_e2m1fn_x4
+ALU = mybir.AluOpType
+AF = mybir.ActivationFunctionType
+
+B, T, E, H, HKV, DH = 4, 1024, 2048, 8, 4, 128
+THETA = 10000.0
+EPS = 1e-6
+P = 128
+G = E // 512
+NT = B * T // P
+TPB = T // P
+HALF = DH // 2
+QS = DH ** -0.5
+
+FLOPS = 2 * B * T * E * (H + 2 * HKV) * DH
+
+Q0, Q1, KK, VV = 0, 1, 2, 3
+W_EVERY = 2
+W_MORE = 16
+NB = 3
+LAGB = 7
+N_PLAIN = 6
+N_SINGLE = 3
+V_FRONT = 0
+V_BACK = 4
+N_WARM = 16
+CHUNKS = ((0, 4), (4, 8), (8, 16), (16, 24), (24, 32))
+
+
+def tile_gemma3mhattention_pa_kernel(
+    tc, x_words, x_scales, wq_words, wq_scales, wk_words, wk_scales, wv_words, wv_scales,
+    q_norm_w, k_norm_w, out_0, out_1, out_2,
+):
+    nc = tc.nc
+    with ExitStack() as ctx:
+        keep = ctx.enter_context(tc.tile_pool(name="keep", bufs=1))
+        small = ctx.enter_context(tc.tile_pool(name="small", bufs=6))
+        work = ctx.enter_context(tc.tile_pool(name="work", bufs=4))
+        prod = ctx.enter_context(tc.tile_pool(name="prod", bufs=3))
+        psum = ctx.enter_context(tc.psum_pool(name="psum", bufs=8))
+        ctx.enter_context(tc.manual_schedule())
+
+        w_src = {
+            Q0: (wq_words[:, :, 0:1024], wq_scales[:, :, 0:512]),
+            Q1: (wq_words[:, :, 1024:2048], wq_scales[:, :, 512:1024]),
+            KK: (wk_words, wk_scales),
+            VV: (wv_words, wv_scales),
+        }
+        wc = {}
+        wp = {}
+        for kind in (VV, KK, Q0, Q1):
+            wc[kind] = keep.tile([P, G, 1024], U8, name="wc%d" % kind, align_bytes=64)
+            wp[kind] = keep.tile([P, G, 512], U8, name="wp%d" % kind, align_bytes=64)
+        xc = []
+        xp = []
+        for c, (ta, tb) in enumerate(CHUNKS):
+            xc.append(keep.tile([P, G, 256 * (tb - ta)], U8, name="xc%d" % c, align_bytes=64))
+            xp.append(keep.tile([P, G, 128 * (tb - ta)], U8, name="xp%d" % c, align_bytes=64))
+
+        def load_planes(planes, scales):
+            for q in range(4):
+                nc.sync.dma_start(
+                    out=planes[32 * q:32 * q + 4, :, :].bitcast(I32),
+                    in_=scales[:, 4 * q:4 * q + 4, :].rearrange("g r n -> r g n").bitcast(I32),
+                )
+
+        def load_codes(codes, words):
+            nc.sync.dma_start(out=codes[:].bitcast(I32), in_=words.rearrange("g p n -> p g n").bitcast(I32))
+
+        def load_x(c):
+            ta, tb = CHUNKS[c]
+            load_planes(xp[c], x_scales[:, :, 128 * ta:128 * tb])
+            load_codes(xc[c], x_words[:, :, 256 * ta:256 * tb])
+
+        def load_w(kind):
+            load_planes(wp[kind], w_src[kind][1])
+            load_codes(wc[kind], w_src[kind][0])
+
+        pos = keep.tile([P, TPB], F32, name="pos")
+        wq_bf = keep.tile([P, DH], BF16, name="wq_bf")
+        wk_bf = keep.tile([P, DH], BF16, name="wk_bf")
+        nc.gpsimd.memset(xp[0][:].bitcast(F32), 0.0)
+        nc.gpsimd.memset(wp[KK][:].bitcast(F32), 0.0)
+        nc.gpsimd.iota(pos[:], pattern=[[P, TPB]], base=0, channel_multiplier=1,
+                       allow_small_or_imprecise_dtypes=True)
+        nc.gpsimd.dma_start(out=wk_bf[:], in_=k_norm_w.partition_broadcast(P))
+        nc.gpsimd.dma_start(out=wq_bf[:], in_=q_norm_w.partition_broadcast(P))
+        for t_ in (wp[Q0], wp[VV], wp[Q1], xp[1]):
+            nc.gpsimd.memset(t_[:].bitcast(F32), 0.0)
+
+        ones = keep.tile([P, 8], F32, name="ones")
+        nc.vector.memset(ones[:], 1.0)
+
+        load_planes(xp[0], x_scales[:, :, 0:128 * CHUNKS[0][1]])
+        load_codes(xc[0], x_words[:, :, 0:256 * CHUNKS[0][1]])
+        load_codes(wc[KK], w_src[KK][0])
+        load_planes(wp[KK], w_src[KK][1])
+        load_w(Q0)
+        load_w(VV)
+        load_w(Q1)
+        load_x(1)
+
+        zeros = keep.tile([P, 512], BF16, name="zeros")
+        nc.vector.memset(zeros[:], 0.0)
+        warm = psum.tile([P, 512], F32, name="ps")
+        for w_ in range(N_WARM):
+            nc.tensor.matmul(out=warm[:], lhsT=zeros[:, 0:P], rhs=zeros[:], start=True, stop=True)
+
+        dummy = keep.tile([P, 2], F32, name="dummy")
+        nc.scalar.activation(out=dummy[:, 0:1], in_=ones[:, 0:1], func=AF.Sin, scale=1.0)
+        fa = keep.tile([P, 8], F32, name="fa")
+        fb = keep.tile([P, 8], F32, name="fb")
+        for a in range(8):
+            nc.scalar.activation(out=fa[:, a:a + 1], in_=ones[:, a:a + 1], func=AF.Copy,
+                                 scale=THETA ** (-(8.0 * a) / HALF) / (2.0 * math.pi))
+            nc.vector.tensor_scalar(out=fb[:, a:a + 1], in0=ones[:, a:a + 1],
+                                    scalar1=THETA ** (-(1.0 * a) / HALF), scalar2=None, op0=ALU.mult)
+        eps_t = keep.tile([P, 1], F32, name="eps_t")
+        nc.scalar.activation(out=eps_t[:], in_=ones[:, 0:1], func=AF.Copy, scale=EPS)
+        freq = keep.tile([P, HALF], F32, name="freq")
+        nc.vector.tensor_tensor(out=freq[:].rearrange("p (a b) -> p a b", a=8),
+                                in0=fa[:].unsqueeze(2).to_broadcast([P, 8, 8]),
+                                in1=fb[:].unsqueeze(1).to_broadcast([P, 8, 8]), op=ALU.mult)
+        ph = keep.tile([P, 2, TPB, HALF], F32, name="ph")
+        nc.vector.tensor_tensor(out=ph[:, 0], in0=pos[:].unsqueeze(2).to_broadcast([P, TPB, HALF]),
+                                in1=freq[:].unsqueeze(1).to_broadcast([P, TPB, HALF]), op=ALU.mult)
+        nc.scalar.activation(out=ph[:, 1], in_=ph[:, 0], func=AF.Copy, scale=1.0, bias=0.25)
+        ni = keep.tile([P, 2, TPB, HALF], I32, name="ni")
+        fr = keep.tile([P, 2, TPB, HALF], F32, name="fr")
+        sc = keep.tile([P, 2, TPB, HALF], F32, name="sc")
+        gains = {}
+        for k, (kind, w_bf, s) in enumerate(((KK, wk_bf, 1.0), (Q0, wq_bf, QS))):
+            nc.vector.tensor_copy(out=ni[:, k], in_=ph[:, k])
+            nc.vector.tensor_tensor(out=fr[:, k], in0=ph[:, k], in1=ni[:, k], op=ALU.subtract)
+            nc.scalar.activation(out=sc[:, k], in_=fr[:, k], func=AF.Sin, scale=2.0 * math.pi)
+            gn = keep.tile([P, DH], F32, name="gn%d" % kind)
+            gs = keep.tile([P, DH], F32, name="gs%d" % kind)
+            nc.scalar.activation(out=gn[:], in_=w_bf[:], func=AF.Copy, scale=s, bias=s)
+            nc.scalar.activation(out=gs[:, 0:HALF], in_=w_bf[:, HALF:DH], func=AF.Copy, scale=-s, bias=-s)
+            nc.scalar.activation(out=gs[:, HALF:DH], in_=w_bf[:, 0:HALF], func=AF.Copy, scale=s, bias=s)
+            gains[kind] = (gn, gs)
+        nc.scalar.activation(out=dummy[:, 1:2], in_=ones[:, 0:1], func=AF.Abs_reciprocal_sqrt, scale=1.0, bias=eps_t[:])
+
+        tabs = {}
+        for kind in (KK, Q0):
+            for half in range(2):
+                ta_ = keep.tile([P, TPB // 2, DH], F32, name="tabA%d%d" % (kind, half))
+                tb_ = keep.tile([P, TPB // 2, DH], F32, name="tabB%d%d" % (kind, half))
+                tabs[(kind, half)] = (ta_, tb_)
+                tabs[(Q1 if kind == Q0 else kind, half)] = (ta_, tb_)
+
+        def build_tables(eng, kind, half):
+            gn, gs = gains[kind]
+            ta_, tb_ = tabs[(kind, half)]
+            n_i = TPB // 2
+            for tab, k, gg in ((tb_, 0, gs), (ta_, 1, gn)):
+                eng.tensor_tensor(
+                    out=tab[:].rearrange("p i (s c) -> p i s c", s=2),
+                    in0=sc[:, k, n_i * half:n_i * (half + 1), :].unsqueeze(2).to_broadcast([P, n_i, 2, HALF]),
+                    in1=gg[:].rearrange("p (s c) -> p s c", s=2).unsqueeze(1).to_broadcast([P, n_i, 2, HALF]),
+                    op=ALU.mult)
+
+        build_tables(nc.vector, KK, 0)
+        build_tables(nc.vector, Q0, 0)
+        build_tables(nc.gpsimd, KK, 1)
+        build_tables(nc.gpsimd, Q0, 1)
+        nc.gpsimd.memset(xp[2][:].bitcast(F32), 0.0)
+
+        def chunk_of(t):
+            for c, (ta, tb) in enumerate(CHUNKS):
+                if ta <= t < tb:
+                    return c, t - ta
+            raise ValueError("token tile out of range")
+
+        def dest(t, kind):
+            b, i = divmod(t, TPB)
+            rows = slice(P * i, P * (i + 1))
+            if kind == Q0:
+                d = out_0[b, 0:4, rows, :]
+            elif kind == Q1:
+                d = out_0[b, 4:8, rows, :]
+            elif kind == KK:
+                d = out_1[b, :, rows, :]
+            else:
+                d = out_2[b, :, rows, :]
+            return d.rearrange("h p c -> p h c")
+
+        qk = []
+        for kind in (KK, Q0, Q1):
+            for t in range(4):
+                qk.append((t, kind))
+        for t in range(4, NT):
+            for kind in (Q0, Q1, KK):
+                qk.append((t, kind))
+        n_mid = NT - V_FRONT - V_BACK
+        seq = []
+        for t in range(V_FRONT):
+            seq.append((t, VV))
+        for j in range(NT):
+            seq.extend(qk[3 * j:3 * j + 3])
+            if (j + 1) * n_mid // NT > j * n_mid // NT and j < NT - 1:
+                seq.append((len(seq) - 3 * (j + 1), VV))
+        for t in range(len(seq) - 3 * NT, NT):
+            seq.append((t, VV))
+        n_qk = 3 * NT
+        sizes = [NB] * ((n_qk - N_SINGLE) // NB) + [1] * N_SINGLE
+        place = []
+        for bi, size in enumerate(sizes):
+            for j in range(size):
+                place.append((bi, j))
+        x_after = {10: 2, 28: 3, 60: 4}
+        zero_after = {2: 3, 5: 4}
+        batch = {}
+        due = {}
+        state = {"q": 0, "pend": None}
+
+        def is_wide(q):
+            return (q % W_EVERY == W_EVERY - 1 or q % W_MORE == 0) and q < n_qk - N_PLAIN
+
+        def products(q, t, kind, ps):
+            bi, j = place[q]
+            bt = batch[bi]
+            i = t % TPB
+            base = 512 * j
+            psv = ps[:].rearrange("p (h s c) -> p h s c", h=4, s=2)
+            ta_, tb_ = tabs[(kind, i // (TPB // 2))]
+            ta1 = ta_[:, i % (TPB // 2), :]
+            tb2 = tb_[:, i % (TPB // 2), :].rearrange("p (s c) -> p s c", s=2)
+            if is_wide(q):
+                nc.vector.tensor_tensor(out=bt["p1"][:, base:base + 512].rearrange("p (h c) -> p h c", h=4),
+                                        in0=ps[:].rearrange("p (h c) -> p h c", h=4),
+                                        in1=ta1.unsqueeze(1).to_broadcast([P, 4, DH]), op=ALU.mult)
+                nc.vector.tensor_tensor(out=bt["p2"][:, base:base + 512].rearrange("p (h s c) -> p h s c", h=4, s=2),
+                                        in0=psv[:, :, ::-1, :],
+                                        in1=tb2.unsqueeze(1).to_broadcast([P, 4, 2, HALF]), op=ALU.mult)
+            else:
+                for h in range(4):
+                    cols = slice(base + DH * h, base + DH * (h + 1))
+                    r = bt["rs"][:, 4 * j + h:4 * j + h + 1]
+                    nc.vector.scalar_tensor_tensor(out=bt["p1"][:, cols], in0=ps[:, DH * h:DH * (h + 1)], scalar=r,
+                                                   in1=ta1, op0=ALU.mult, op1=ALU.mult)
+                    nc.vector.scalar_tensor_tensor(out=bt["p2"][:, cols].rearrange("p (s c) -> p s c", s=2),
+                                                   in0=psv[:, h, ::-1, :], scalar=r,
+                                                   in1=tb2, op0=ALU.mult, op1=ALU.mult)
+            bt["done"] += 1
+
+        def maybe_add(bi, step):
+            bt = batch[bi]
+            if bt["done"] < sizes[bi] or bt["added"]:
+                return
+            w = 512 * sizes[bi]
+            ob = work.tile([P, 512 * NB], F32, name="ob", bufs=6)
+            nc.gpsimd.tensor_tensor(out=ob[:, 0:w], in0=bt["p1"][:, 0:w], in1=bt["p2"][:, 0:w], op=ALU.add)
+            bt["ob"] = ob
+            bt["added"] = True
+            if bi in zero_after:
+                nc.gpsimd.memset(xp[zero_after[bi]][:].bitcast(F32), 0.0)
+            lag = LAGB if sizes[bi] > 1 else 4
+            due.setdefault(step + lag, []).append(bi)
+
+        def finish(bi):
+            bt = batch[bi]
+            for j, (q, t, kind) in enumerate(bt["members"]):
+                base = 512 * j
+                if is_wide(q):
+                    for h in range(4):
+                        cols = slice(base + DH * h, base + DH * (h + 1))
+                        nc.scalar.activation(out=bt["ob"][:, cols], in_=bt["ob"][:, cols], func=AF.Copy,
+                                             scale=bt["rs"][:, 4 * j + h:4 * j + h + 1])
+                nc.sync.dma_start(out=dest(t, kind),
+                                  in_=bt["ob"][:, base:base + 512].rearrange("p (h c) -> p h c", h=4))
+
+        def rsqrt_and_products(step):
+            if state["pend"] is None:
+                return
+            q, t, kind, ps = state["pend"]
+            state["pend"] = None
+            bi, j = place[q]
+            bt = batch[bi]
+            nc.scalar.activation(out=bt["rs"][:, 4 * j:4 * j + 4], in_=bt["ss"][:, 4 * j:4 * j + 4],
+                                 func=AF.Abs_reciprocal_sqrt, scale=1.0 / DH, bias=eps_t[:])
+            if not is_wide(q):
+                products(q, t, kind, ps)
+            maybe_add(bi, step)
+
+        last = len(seq) + LAGB + 2
+        for step in range(last):
+            if step < len(seq):
+                t, kind = seq[step]
+                c, tl = chunk_of(t)
+                ps = psum.tile([P, 512], F32, name="ps")
+                for g in range(G):
+                    nc.tensor.matmul_mx(
+                        out=ps[:],
+                        lhsT=xc[c][:, g, 256 * tl:256 * (tl + 1)].bitcast(FP4X4),
+                        lhsT_scale=xp[c][:, g, 128 * tl:128 * (tl + 1)],
+                        rhs=wc[kind][:, g, :].bitcast(FP4X4),
+                        rhs_scale=wp[kind][:, g, :],
+                        start=(g == 0), stop=(g == G - 1),
+                    )
+                if kind == VV:
+                    vo = work.tile([P, 512], F32, name="vo")
+                    nc.scalar.copy(out=vo[:], in_=ps[:])
+                    nc.sync.dma_start(out=dest(t, kind), in_=vo[:].rearrange("p (h c) -> p h c", h=4))
+                    rsqrt_and_products(step)
+                else:
+                    q = state["q"]
+                    state["q"] = q + 1
+                    bi, j = place[q]
+                    if j == 0:
+                        ssb = small.tile([P, 4 * NB], F32, name="ssb")
+                        rsb = small.tile([P, 4 * NB], F32, name="rsb")
+                        p1b = prod.tile([P, 512 * NB], F32, name="p1b")
+                        p2b = prod.tile([P, 512 * NB], F32, name="p2b")
+                        batch[bi] = {"ss": ssb, "rs": rsb, "p1": p1b, "p2": p2b, "done": 0, "added": False, "members": []}
+                    bt = batch[bi]
+                    bt["members"].append((q, t, kind))
+                    for h in range(4):
+                        junk = small.tile([P, DH], F32, name="junk")
+                        nc.scalar.activation(out=junk[:], in_=ps[:, DH * h:DH * (h + 1)], func=AF.Square,
+                                             accum_out=bt["ss"][:, 4 * j + h:4 * j + h + 1])
+                    rsqrt_and_products(step)
+                    if is_wide(q):
+                        products(q, t, kind, ps)
+                    state["pend"] = (q, t, kind, ps)
+                    if q >= n_qk - N_SINGLE:
+                        rsqrt_and_products(step)
+            else:
+                rsqrt_and_products(step)
+            for bi in due.get(step, []):
+                finish(bi)
+            if step in x_after:
+                load_x(x_after[step])

@@ -153,18 +153,17 @@ def tile_gemma3mhattention_pa_kernel(
         tabs = {}
         for kind in (KK, Q0):
             for half in range(2):
-                ta_ = keep.tile([P, TPB // 2, DH], F32, name="tabA%d%d" % (kind, half))
-                tb_ = keep.tile([P, TPB // 2, DH], F32, name="tabB%d%d" % (kind, half))
-                tabs[(kind, half)] = (ta_, tb_)
-                tabs[(Q1 if kind == Q0 else kind, half)] = (ta_, tb_)
+                tab_ = keep.tile([P, TPB // 2, 2 * DH], F32, name="tab%d%d" % (kind, half))
+                tabs[(kind, half)] = tab_
+                tabs[(Q1 if kind == Q0 else kind, half)] = tab_
 
         def build_tables(eng, kind, half):
             gn, gs = gains[kind]
-            ta_, tb_ = tabs[(kind, half)]
+            blocks = tabs[(kind, half)][:].rearrange("p i (b c) -> p i b c", b=4)
             n_i = TPB // 2
-            for tab, k, gg in ((tb_, 0, gs), (ta_, 1, gn)):
+            for sel, k, gg in ((slice(1, 3), 0, gs), (slice(0, 4, 3), 1, gn)):
                 eng.tensor_tensor(
-                    out=tab[:].rearrange("p i (s c) -> p i s c", s=2),
+                    out=blocks[:, :, sel, :],
                     in0=sc[:, k, n_i * half:n_i * (half + 1), :].unsqueeze(2).to_broadcast([P, n_i, 2, HALF]),
                     in1=gg[:].rearrange("p (s c) -> p s c", s=2).unsqueeze(1).to_broadcast([P, n_i, 2, HALF]),
                     op=ALU.mult)
@@ -230,27 +229,19 @@ def tile_gemma3mhattention_pa_kernel(
             bi, j = place[q]
             bt = batch[bi]
             i = t % TPB
-            base = 512 * j
-            psv = ps[:].rearrange("p (h s c) -> p h s c", h=4, s=2)
-            ta_, tb_ = tabs[(kind, i // (TPB // 2))]
-            ta1 = ta_[:, i % (TPB // 2), :]
-            tb2 = tb_[:, i % (TPB // 2), :].rearrange("p (s c) -> p s c", s=2)
+            base = 1024 * j
+            tab = tabs[(kind, i // (TPB // 2))][:, i % (TPB // 2), :].rearrange("p (s c) -> p s c", s=2)
             if is_wide(q):
-                nc.vector.tensor_tensor(out=bt["p1"][:, base:base + 512].rearrange("p (h c) -> p h c", h=4),
-                                        in0=ps[:].rearrange("p (h c) -> p h c", h=4),
-                                        in1=ta1.unsqueeze(1).to_broadcast([P, 4, DH]), op=ALU.mult)
-                nc.vector.tensor_tensor(out=bt["p2"][:, base:base + 512].rearrange("p (h s c) -> p h s c", h=4, s=2),
-                                        in0=psv[:, :, ::-1, :],
-                                        in1=tb2.unsqueeze(1).to_broadcast([P, 4, 2, HALF]), op=ALU.mult)
+                nc.vector.tensor_tensor(out=bt["pp"][:, base:base + 1024].rearrange("p (h s c) -> p h s c", h=4, s=2),
+                                        in0=ps[:].rearrange("p (h c) -> p h c", h=4).unsqueeze(2).to_broadcast([P, 4, 2, DH]),
+                                        in1=tab.unsqueeze(1).to_broadcast([P, 4, 2, DH]), op=ALU.mult)
             else:
                 for h in range(4):
-                    cols = slice(base + DH * h, base + DH * (h + 1))
                     r = bt["rs"][:, 4 * j + h:4 * j + h + 1]
-                    nc.vector.scalar_tensor_tensor(out=bt["p1"][:, cols], in0=ps[:, DH * h:DH * (h + 1)], scalar=r,
-                                                   in1=ta1, op0=ALU.mult, op1=ALU.mult)
-                    nc.vector.scalar_tensor_tensor(out=bt["p2"][:, cols].rearrange("p (s c) -> p s c", s=2),
-                                                   in0=psv[:, h, ::-1, :], scalar=r,
-                                                   in1=tb2, op0=ALU.mult, op1=ALU.mult)
+                    nc.vector.scalar_tensor_tensor(
+                        out=bt["pp"][:, base + 2 * DH * h:base + 2 * DH * (h + 1)].rearrange("p (s c) -> p s c", s=2),
+                        in0=ps[:, DH * h:DH * (h + 1)].unsqueeze(1).to_broadcast([P, 2, DH]), scalar=r,
+                        in1=tab, op0=ALU.mult, op1=ALU.mult)
             bt["done"] += 1
 
         def maybe_add(bi, step):
@@ -259,7 +250,9 @@ def tile_gemma3mhattention_pa_kernel(
                 return
             w = 512 * sizes[bi]
             ob = work.tile([P, 512 * NB], F32, name="ob", bufs=6)
-            nc.gpsimd.tensor_tensor(out=ob[:, 0:w], in0=bt["p1"][:, 0:w], in1=bt["p2"][:, 0:w], op=ALU.add)
+            ppv = bt["pp"][:, 0:2 * w].rearrange("p (m k c) -> p m k c", k=2, c=HALF)
+            nc.gpsimd.tensor_tensor(out=ob[:, 0:w].rearrange("p (m c) -> p m c", c=HALF),
+                                    in0=ppv[:, :, 0, :], in1=ppv[:, :, 1, :], op=ALU.add)
             bt["ob"] = ob
             bt["added"] = True
             if bi in zero_after:
@@ -319,9 +312,8 @@ def tile_gemma3mhattention_pa_kernel(
                     if j == 0:
                         ssb = small.tile([P, 4 * NB], F32, name="ssb")
                         rsb = small.tile([P, 4 * NB], F32, name="rsb")
-                        p1b = prod.tile([P, 512 * NB], F32, name="p1b")
-                        p2b = prod.tile([P, 512 * NB], F32, name="p2b")
-                        batch[bi] = {"ss": ssb, "rs": rsb, "p1": p1b, "p2": p2b, "done": 0, "added": False, "members": []}
+                        ppb = prod.tile([P, 1024 * NB], F32, name="ppb")
+                        batch[bi] = {"ss": ssb, "rs": rsb, "pp": ppb, "done": 0, "added": False, "members": []}
                     bt = batch[bi]
                     bt["members"].append((q, t, kind))
                     for h in range(4):

@@ -24,8 +24,7 @@ QS = DH ** -0.5
 FLOPS = 2 * B * T * E * (H + 2 * HKV) * DH
 
 Q0, Q1, KK, VV = 0, 1, 2, 3
-W_EVERY = 2
-W_MORE = 16
+N_WIDE = 0
 NB = 3
 LAGB = 7
 N_PLAIN = 6
@@ -223,7 +222,7 @@ def tile_gemma3mhattention_pa_kernel(
         state = {"q": 0, "pend": None}
 
         def is_wide(q):
-            return (q % W_EVERY == W_EVERY - 1 or q % W_MORE == 0) and q < n_qk - N_PLAIN
+            return (q + 1) * N_WIDE // n_qk > q * N_WIDE // n_qk and q < n_qk - N_PLAIN
 
         def products(q, t, kind, ps):
             bi, j = place[q]

@@ -85,24 +85,25 @@ def tile_gemma3mhattention_pa_kernel(
             load_codes(wc[kind], w_src[kind][0])
 
         pos = keep.tile([P, TPB], F32, name="pos")
-        wq_bf = keep.tile([P, DH], BF16, name="wq_bf")
-        wk_bf = keep.tile([P, DH], BF16, name="wk_bf")
+        wrow = keep.tile([P, 2 * DH], BF16, name="wrow")
+        ones_bf = keep.tile([P, P], BF16, name="ones_bf")
+        nc.vector.memset(wrow[:], 0.0)
         nc.gpsimd.memset(xp[0][:].bitcast(F32), 0.0)
         nc.gpsimd.memset(wp[KK][:].bitcast(F32), 0.0)
         nc.gpsimd.iota(pos[:], pattern=[[P, TPB]], base=0, channel_multiplier=1,
                        allow_small_or_imprecise_dtypes=True)
-        nc.gpsimd.dma_start(out=wk_bf[:], in_=k_norm_w.partition_broadcast(P))
-        nc.gpsimd.dma_start(out=wq_bf[:], in_=q_norm_w.partition_broadcast(P))
         for t_ in (wp[Q0], wp[VV], wp[Q1], xp[1]):
             nc.gpsimd.memset(t_[:].bitcast(F32), 0.0)
 
         ones = keep.tile([P, 8], F32, name="ones")
         nc.vector.memset(ones[:], 1.0)
 
+        nc.sync.dma_start(out=wrow[0:1, 0:DH], in_=k_norm_w.unsqueeze(0))
         load_planes(xp[0], x_scales[:, :, 0:128 * CHUNKS[0][1]])
         load_codes(xc[0], x_words[:, :, 0:256 * CHUNKS[0][1]])
         load_codes(wc[KK], w_src[KK][0])
         load_planes(wp[KK], w_src[KK][1])
+        nc.sync.dma_start(out=wrow[0:1, DH:2 * DH], in_=q_norm_w.unsqueeze(0))
         load_w(Q0)
         load_w(VV)
         load_w(Q1)
@@ -110,8 +111,17 @@ def tile_gemma3mhattention_pa_kernel(
 
         zeros = keep.tile([P, 512], BF16, name="zeros")
         nc.vector.memset(zeros[:], 0.0)
+        nc.vector.memset(ones_bf[:], 1.0)
         warm = psum.tile([P, 512], F32, name="ps")
+
+        def spread(c0):
+            wps = psum.tile([P, 512], F32, name="ps")
+            nc.tensor.matmul(out=wps[:, 0:DH], lhsT=ones_bf[:], rhs=wrow[:, c0:c0 + DH], start=True, stop=True)
+            return wps[:, 0:DH]
+
         for w_ in range(N_WARM):
+            if w_ == N_WARM // 2:
+                wk_ps = spread(0)
             nc.tensor.matmul(out=warm[:], lhsT=zeros[:, 0:P], rhs=zeros[:], start=True, stop=True)
 
         dummy = keep.tile([P, 2], F32, name="dummy")
@@ -137,16 +147,20 @@ def tile_gemma3mhattention_pa_kernel(
         fr = keep.tile([P, 2, TPB, HALF], F32, name="fr")
         sc = keep.tile([P, 2, TPB, HALF], F32, name="sc")
         gains = {}
-        for k, (kind, w_bf, s) in enumerate(((KK, wk_bf, 1.0), (Q0, wq_bf, QS))):
+        for k in range(2):
             nc.vector.tensor_copy(out=ni[:, k], in_=ph[:, k])
             nc.vector.tensor_tensor(out=fr[:, k], in0=ph[:, k], in1=ni[:, k], op=ALU.subtract)
             nc.scalar.activation(out=sc[:, k], in_=fr[:, k], func=AF.Sin, scale=2.0 * math.pi)
+
+        def make_gains(kind, w_bf, s):
             gn = keep.tile([P, DH], F32, name="gn%d" % kind)
             gs = keep.tile([P, DH], F32, name="gs%d" % kind)
-            nc.scalar.activation(out=gn[:], in_=w_bf[:], func=AF.Copy, scale=s, bias=s)
+            nc.scalar.activation(out=gn[:], in_=w_bf, func=AF.Copy, scale=s, bias=s)
             nc.scalar.activation(out=gs[:, 0:HALF], in_=w_bf[:, HALF:DH], func=AF.Copy, scale=-s, bias=-s)
             nc.scalar.activation(out=gs[:, HALF:DH], in_=w_bf[:, 0:HALF], func=AF.Copy, scale=s, bias=s)
             gains[kind] = (gn, gs)
+
+        make_gains(KK, wk_ps, 1.0)
         nc.scalar.activation(out=dummy[:, 1:2], in_=ones[:, 0:1], func=AF.Abs_reciprocal_sqrt, scale=1.0, bias=eps_t[:])
 
         tabs = {}
@@ -168,9 +182,7 @@ def tile_gemma3mhattention_pa_kernel(
                     op=ALU.mult)
 
         build_tables(nc.vector, KK, 0)
-        build_tables(nc.vector, Q0, 0)
         build_tables(nc.gpsimd, KK, 1)
-        build_tables(nc.gpsimd, Q0, 1)
         nc.gpsimd.memset(xp[2][:].bitcast(F32), 0.0)
 
         def chunk_of(t):
@@ -299,6 +311,8 @@ def tile_gemma3mhattention_pa_kernel(
                         rhs_scale=wp[kind][:, g, :],
                         start=(g == 0), stop=(g == G - 1),
                     )
+                if step == 0:
+                    wq_ps = spread(DH)
                 if kind == VV:
                     vo = work.tile([P, 512], F32, name="vo")
                     nc.scalar.copy(out=vo[:], in_=ps[:])
@@ -319,6 +333,10 @@ def tile_gemma3mhattention_pa_kernel(
                         junk = small.tile([P, DH], F32, name="junk")
                         nc.scalar.activation(out=junk[:], in_=ps[:, DH * h:DH * (h + 1)], func=AF.Square,
                                              accum_out=bt["ss"][:, 4 * j + h:4 * j + h + 1])
+                    if step == 0:
+                        make_gains(Q0, wq_ps, QS)
+                        build_tables(nc.vector, Q0, 0)
+                        build_tables(nc.gpsimd, Q0, 1)
                     rsqrt_and_products(step)
                     if is_wide(q):
                         products(q, t, kind, ps)

@@ -30,7 +30,7 @@ LAGB = 7
 N_PLAIN = 6
 N_SINGLE = 3
 V_FRONT = 0
-V_BACK = 4
+V_BACK = 6
 N_WARM = 16
 CHUNKS = ((0, 4), (4, 8), (8, 16), (16, 24), (24, 32))
 
@@ -98,10 +98,10 @@ def tile_gemma3mhattention_pa_kernel(
         ones = keep.tile([P, 8], F32, name="ones")
         nc.vector.memset(ones[:], 1.0)
 
-        nc.sync.dma_start(out=wrow[0:1, 0:DH], in_=k_norm_w.unsqueeze(0))
-        load_planes(xp[0], x_scales[:, :, 0:128 * CHUNKS[0][1]])
         load_codes(xc[0], x_words[:, :, 0:256 * CHUNKS[0][1]])
         load_codes(wc[KK], w_src[KK][0])
+        nc.sync.dma_start(out=wrow[0:1, 0:DH], in_=k_norm_w.unsqueeze(0))
+        load_planes(xp[0], x_scales[:, :, 0:128 * CHUNKS[0][1]])
         load_planes(wp[KK], w_src[KK][1])
         nc.sync.dma_start(out=wrow[0:1, DH:2 * DH], in_=q_norm_w.unsqueeze(0))
         load_w(Q0)
@@ -301,19 +301,33 @@ def tile_gemma3mhattention_pa_kernel(
             if step < len(seq):
                 t, kind = seq[step]
                 c, tl = chunk_of(t)
-                ps = psum.tile([P, 512], F32, name="ps")
-                for g in range(G):
-                    nc.tensor.matmul_mx(
-                        out=ps[:],
-                        lhsT=xc[c][:, g, 256 * tl:256 * (tl + 1)].bitcast(FP4X4),
-                        lhsT_scale=xp[c][:, g, 128 * tl:128 * (tl + 1)],
-                        rhs=wc[kind][:, g, :].bitcast(FP4X4),
-                        rhs_scale=wp[kind][:, g, :],
-                        start=(g == 0), stop=(g == G - 1),
-                    )
+                widths = [512] if step < len(seq) - 1 else [DH] * 4
+                banks = []
+                for n_, wd in enumerate(widths):
+                    ps = psum.tile([P, 512], F32, name="ps")
+                    banks.append(ps)
+                    for g in range(G):
+                        nc.tensor.matmul_mx(
+                            out=ps[:, 0:wd],
+                            lhsT=xc[c][:, g, 256 * tl:256 * (tl + 1)].bitcast(FP4X4),
+                            lhsT_scale=xp[c][:, g, 128 * tl:128 * (tl + 1)],
+                            rhs=wc[kind][:, g, 2 * wd * n_:2 * wd * (n_ + 1)].bitcast(FP4X4),
+                            rhs_scale=wp[kind][:, g, wd * n_:wd * (n_ + 1)],
+                            start=(g == 0), stop=(g == G - 1),
+                        )
                 if step == 0:
                     wq_ps = spread(DH)
-                if kind == VV:
+                if len(banks) > 1:
+                    vo = work.tile([P, 512], F32, name="vo")
+                    for h, ps in enumerate(banks):
+                        cols = slice(DH * h, DH * (h + 1))
+                        if h % 2 == 0:
+                            nc.scalar.copy(out=vo[:, cols], in_=ps[:, 0:DH])
+                        else:
+                            nc.vector.tensor_copy(out=vo[:, cols], in_=ps[:, 0:DH])
+                        nc.sync.dma_start(out=dest(t, kind)[:, h, :], in_=vo[:, cols])
+                    rsqrt_and_products(step)
+                elif kind == VV:
                     vo = work.tile([P, 512], F32, name="vo")
                     nc.scalar.copy(out=vo[:], in_=ps[:])
                     nc.sync.dma_start(out=dest(t, kind), in_=vo[:].rearrange("p (h c) -> p h c", h=4))

@@ -31,7 +31,7 @@ N_PLAIN = 6
 N_SINGLE = 3
 V_FRONT = 0
 V_BACK = 6
-N_WARM = 16
+N_WARM = 10
 CHUNKS = ((0, 4), (4, 8), (8, 16), (16, 24), (24, 32))
 
 

@@ -57,13 +57,13 @@ def tile_gemma3mhattention_pa_kernel(
         wc = {}
         wp = {}
         for kind in (VV, KK, Q0, Q1):
-            wc[kind] = keep.tile([P, G, 1024], U8, name="wc%d" % kind, align_bytes=64)
-            wp[kind] = keep.tile([P, G, 512], U8, name="wp%d" % kind, align_bytes=64)
+            wc[kind] = keep.tile([P, G, 1024], U8, name="wc%d" % kind, align_bytes=256)
+            wp[kind] = keep.tile([P, G, 512], U8, name="wp%d" % kind, align_bytes=256)
         xc = []
         xp = []
         for c, (ta, tb) in enumerate(CHUNKS):
-            xc.append(keep.tile([P, G, 256 * (tb - ta)], U8, name="xc%d" % c, align_bytes=64))
-            xp.append(keep.tile([P, G, 128 * (tb - ta)], U8, name="xp%d" % c, align_bytes=64))
+            xc.append(keep.tile([P, G, 256 * (tb - ta)], U8, name="xc%d" % c, align_bytes=256))
+            xp.append(keep.tile([P, G, 128 * (tb - ta)], U8, name="xp%d" % c, align_bytes=256))
 
         def load_planes(planes, scales):
             for q in range(4):

@@ -166,7 +166,7 @@ def tile_gemma3mhattention_pa_kernel(
         tabs = {}
         for kind in (KK, Q0):
             for half in range(2):
-                tab_ = keep.tile([P, TPB // 2, 2 * DH], F32, name="tab%d%d" % (kind, half))
+                tab_ = keep.tile([P, TPB // 2, 2 * DH], F32, name="tab%d%d" % (kind, half), align_bytes=256)
                 tabs[(kind, half)] = tab_
                 tabs[(Q1 if kind == Q0 else kind, half)] = tab_
 
@@ -260,7 +260,7 @@ def tile_gemma3mhattention_pa_kernel(
             if bt["done"] < sizes[bi] or bt["added"]:
                 return
             w = 512 * sizes[bi]
-            ob = work.tile([P, 512 * NB], F32, name="ob", bufs=6)
+            ob = work.tile([P, 512 * NB], F32, name="ob", bufs=6, align_bytes=256)
             ppv = bt["pp"][:, 0:2 * w].rearrange("p (m k c) -> p m k c", k=2, c=HALF)
             nc.gpsimd.tensor_tensor(out=ob[:, 0:w].rearrange("p (m c) -> p m c", c=HALF),
                                     in0=ppv[:, :, 0, :], in1=ppv[:, :, 1, :], op=ALU.add)
@@ -318,7 +318,7 @@ def tile_gemma3mhattention_pa_kernel(
                 if step == 0:
                     wq_ps = spread(DH)
                 if len(banks) > 1:
-                    vo = work.tile([P, 512], F32, name="vo")
+                    vo = work.tile([P, 512], F32, name="vo", align_bytes=256)
                     for h, ps in enumerate(banks):
                         cols = slice(DH * h, DH * (h + 1))
                         if h % 2 == 0:
@@ -328,7 +328,7 @@ def tile_gemma3mhattention_pa_kernel(
                         nc.sync.dma_start(out=dest(t, kind)[:, h, :], in_=vo[:, cols])
                     rsqrt_and_products(step)
                 elif kind == VV:
-                    vo = work.tile([P, 512], F32, name="vo")
+                    vo = work.tile([P, 512], F32, name="vo", align_bytes=256)
                     nc.scalar.copy(out=vo[:], in_=ps[:])
                     nc.sync.dma_start(out=dest(t, kind), in_=vo[:].rearrange("p (h c) -> p h c", h=4))
                     rsqrt_and_products(step)
@@ -339,12 +339,12 @@ def tile_gemma3mhattention_pa_kernel(
                     if j == 0:
                         ssb = small.tile([P, 4 * NB], F32, name="ssb")
                         rsb = small.tile([P, 4 * NB], F32, name="rsb")
-                        ppb = prod.tile([P, 1024 * NB], F32, name="ppb")
+                        ppb = prod.tile([P, 1024 * NB], F32, name="ppb", align_bytes=256)
                         batch[bi] = {"ss": ssb, "rs": rsb, "pp": ppb, "done": 0, "added": False, "members": []}
                     bt = batch[bi]
                     bt["members"].append((q, t, kind))
                     for h in range(4):
-                        junk = small.tile([P, DH], F32, name="junk")
+                        junk = small.tile([P, DH], F32, name="junk", align_bytes=256)
                         nc.scalar.activation(out=junk[:], in_=ps[:, DH * h:DH * (h + 1)], func=AF.Square,
                                              accum_out=bt["ss"][:, 4 * j + h:4 * j + h + 1])
                     if step == 0:

@@ -33,6 +33,7 @@ V_FRONT = 0
 V_BACK = 6
 N_WARM = 10
 CHUNKS = ((0, 4), (4, 8), (8, 16), (16, 24), (24, 32))
+CODE_CHUNKS = ((0, 2), (2, 4)) + CHUNKS[1:]
 
 
 def tile_gemma3mhattention_pa_kernel(
@@ -61,8 +62,9 @@ def tile_gemma3mhattention_pa_kernel(
             wp[kind] = keep.tile([P, G, 512], U8, name="wp%d" % kind, align_bytes=256)
         xc = []
         xp = []
-        for c, (ta, tb) in enumerate(CHUNKS):
+        for c, (ta, tb) in enumerate(CODE_CHUNKS):
             xc.append(keep.tile([P, G, 256 * (tb - ta)], U8, name="xc%d" % c, align_bytes=256))
+        for c, (ta, tb) in enumerate(CHUNKS):
             xp.append(keep.tile([P, G, 128 * (tb - ta)], U8, name="xp%d" % c, align_bytes=256))
 
         def load_planes(planes, scales):
@@ -75,10 +77,14 @@ def tile_gemma3mhattention_pa_kernel(
         def load_codes(codes, words):
             nc.sync.dma_start(out=codes[:].bitcast(I32), in_=words.rearrange("g p n -> p g n").bitcast(I32))
 
+        def load_x_codes(c):
+            ta, tb = CODE_CHUNKS[c]
+            load_codes(xc[c], x_words[:, :, 256 * ta:256 * tb])
+
         def load_x(c):
             ta, tb = CHUNKS[c]
             load_planes(xp[c], x_scales[:, :, 128 * ta:128 * tb])
-            load_codes(xc[c], x_words[:, :, 256 * ta:256 * tb])
+            load_x_codes(c + 1)
 
         def load_w(kind):
             load_planes(wp[kind], w_src[kind][1])
@@ -98,11 +104,12 @@ def tile_gemma3mhattention_pa_kernel(
         ones = keep.tile([P, 8], F32, name="ones")
         nc.vector.memset(ones[:], 1.0)
 
-        load_codes(xc[0], x_words[:, :, 0:256 * CHUNKS[0][1]])
+        load_x_codes(0)
         load_codes(wc[KK], w_src[KK][0])
         nc.sync.dma_start(out=wrow[0:1, 0:DH], in_=k_norm_w.unsqueeze(0))
         load_planes(xp[0], x_scales[:, :, 0:128 * CHUNKS[0][1]])
         load_planes(wp[KK], w_src[KK][1])
+        load_x_codes(1)
         nc.sync.dma_start(out=wrow[0:1, DH:2 * DH], in_=q_norm_w.unsqueeze(0))
         load_w(Q0)
         load_w(VV)
@@ -185,8 +192,8 @@ def tile_gemma3mhattention_pa_kernel(
         build_tables(nc.gpsimd, KK, 1)
         nc.gpsimd.memset(xp[2][:].bitcast(F32), 0.0)
 
-        def chunk_of(t):
-            for c, (ta, tb) in enumerate(CHUNKS):
+        def chunk_of(chunks, t):
+            for c, (ta, tb) in enumerate(chunks):
                 if ta <= t < tb:
                     return c, t - ta
             raise ValueError("token tile out of range")
@@ -300,7 +307,8 @@ def tile_gemma3mhattention_pa_kernel(
         for step in range(last):
             if step < len(seq):
                 t, kind = seq[step]
-                c, tl = chunk_of(t)
+                c, tl = chunk_of(CHUNKS, t)
+                cc, tc_ = chunk_of(CODE_CHUNKS, t)
                 widths = [512] if step < len(seq) - 1 else [DH] * 4
                 banks = []
                 for n_, wd in enumerate(widths):
@@ -309,7 +317,7 @@ def tile_gemma3mhattention_pa_kernel(
                     for g in range(G):
                         nc.tensor.matmul_mx(
                             out=ps[:, 0:wd],
-                            lhsT=xc[c][:, g, 256 * tl:256 * (tl + 1)].bitcast(FP4X4),
+                            lhsT=xc[cc][:, g, 256 * tc_:256 * (tc_ + 1)].bitcast(FP4X4),
                             lhsT_scale=xp[c][:, g, 128 * tl:128 * (tl + 1)],
                             rhs=wc[kind][:, g, 2 * wd * n_:2 * wd * (n_ + 1)].bitcast(FP4X4),
                             rhs_scale=wp[kind][:, g, wd * n_:wd * (n_ + 1)],

@@ -28,7 +28,8 @@ N_WIDE = 0
 NB = 3
 LAGB = 7
 N_PLAIN = 6
-N_SINGLE = 3
+N_SINGLE = 24
+N_NOW = 3
 V_FRONT = 0
 V_BACK = 6
 N_WARM = 10
@@ -267,7 +268,10 @@ def tile_gemma3mhattention_pa_kernel(
             if bt["done"] < sizes[bi] or bt["added"]:
                 return
             w = 512 * sizes[bi]
-            ob = work.tile([P, 512 * NB], F32, name="ob", bufs=6, align_bytes=256)
+            if sizes[bi] > 1:
+                ob = work.tile([P, 512 * NB], F32, name="ob", bufs=6, align_bytes=256)
+            else:
+                ob = work.tile([P, 512], F32, name="ob1", bufs=8, align_bytes=256)
             ppv = bt["pp"][:, 0:2 * w].rearrange("p (m k c) -> p m k c", k=2, c=HALF)
             nc.gpsimd.tensor_tensor(out=ob[:, 0:w].rearrange("p (m c) -> p m c", c=HALF),
                                     in0=ppv[:, :, 0, :], in1=ppv[:, :, 1, :], op=ALU.add)
@@ -347,7 +351,10 @@ def tile_gemma3mhattention_pa_kernel(
                     if j == 0:
                         ssb = small.tile([P, 4 * NB], F32, name="ssb")
                         rsb = small.tile([P, 4 * NB], F32, name="rsb")
-                        ppb = prod.tile([P, 1024 * NB], F32, name="ppb", align_bytes=256)
+                        if sizes[bi] > 1:
+                            ppb = prod.tile([P, 1024 * NB], F32, name="ppb", align_bytes=256)
+                        else:
+                            ppb = prod.tile([P, 1024], F32, name="pp1", bufs=5, align_bytes=256)
                         batch[bi] = {"ss": ssb, "rs": rsb, "pp": ppb, "done": 0, "added": False, "members": []}
                     bt = batch[bi]
                     bt["members"].append((q, t, kind))
@@ -363,7 +370,7 @@ def tile_gemma3mhattention_pa_kernel(
                     if is_wide(q):
                         products(q, t, kind, ps)
                     state["pend"] = (q, t, kind, ps)
-                    if q >= n_qk - N_SINGLE:
+                    if q >= n_qk - N_NOW:
                         rsqrt_and_products(step)
             else:
                 rsqrt_and_products(step)

@@ -32,9 +32,10 @@ N_SINGLE = 24
 N_NOW = 3
 V_FRONT = 0
 V_BACK = 6
-N_WARM = 10
+N_WARM = 8
 CHUNKS = ((0, 4), (4, 8), (8, 16), (16, 24), (24, 32))
 CODE_CHUNKS = ((0, 2), (2, 4)) + CHUNKS[1:]
+HG = G // 2
 
 
 def tile_gemma3mhattention_pa_kernel(
@@ -59,12 +60,21 @@ def tile_gemma3mhattention_pa_kernel(
         wc = {}
         wp = {}
         for kind in (VV, KK, Q0, Q1):
-            wc[kind] = keep.tile([P, G, 1024], U8, name="wc%d" % kind, align_bytes=256)
+            if kind != KK:
+                wc[kind] = keep.tile([P, G, 1024], U8, name="wc%d" % kind, align_bytes=256)
             wp[kind] = keep.tile([P, G, 512], U8, name="wp%d" % kind, align_bytes=256)
+        xh = []
+        wkh = []
+        for hf in range(2):
+            xh.append(keep.tile([P, HG, 512], U8, name="xh%d" % hf, align_bytes=256))
+            wkh.append(keep.tile([P, HG, 1024], U8, name="wkh%d" % hf, align_bytes=256))
         xc = []
         xp = []
         for c, (ta, tb) in enumerate(CODE_CHUNKS):
-            xc.append(keep.tile([P, G, 256 * (tb - ta)], U8, name="xc%d" % c, align_bytes=256))
+            if c == 0:
+                xc.append(None)
+            else:
+                xc.append(keep.tile([P, G, 256 * (tb - ta)], U8, name="xc%d" % c, align_bytes=256))
         for c, (ta, tb) in enumerate(CHUNKS):
             xp.append(keep.tile([P, G, 128 * (tb - ta)], U8, name="xp%d" % c, align_bytes=256))
 
@@ -105,13 +115,15 @@ def tile_gemma3mhattention_pa_kernel(
         ones = keep.tile([P, 8], F32, name="ones")
         nc.vector.memset(ones[:], 1.0)
 
-        load_x_codes(0)
-        load_codes(wc[KK], w_src[KK][0])
+        load_codes(xh[0], x_words[0:HG, :, 0:512])
+        load_codes(wkh[0], wk_words[0:HG])
         nc.sync.dma_start(out=wrow[0:1, 0:DH], in_=k_norm_w.unsqueeze(0))
         load_planes(xp[0], x_scales[:, :, 0:128 * CHUNKS[0][1]])
         load_planes(wp[KK], w_src[KK][1])
-        load_x_codes(1)
         nc.sync.dma_start(out=wrow[0:1, DH:2 * DH], in_=q_norm_w.unsqueeze(0))
+        load_codes(xh[1], x_words[HG:G, :, 0:512])
+        load_codes(wkh[1], wk_words[HG:G])
+        load_x_codes(1)
         load_w(Q0)
         load_w(VV)
         load_w(Q1)
@@ -240,6 +252,7 @@ def tile_gemma3mhattention_pa_kernel(
         batch = {}
         due = {}
         state = {"q": 0, "pend": None}
+        first = {}
 
         def is_wide(q):
             return (q + 1) * N_WIDE // n_qk > q * N_WIDE // n_qk and q < n_qk - N_PLAIN
@@ -315,15 +328,41 @@ def tile_gemma3mhattention_pa_kernel(
                 cc, tc_ = chunk_of(CODE_CHUNKS, t)
                 widths = [512] if step < len(seq) - 1 else [DH] * 4
                 banks = []
+                if step == 0:
+                    for s_ in range(2):
+                        first[s_] = psum.tile([P, 512], F32, name="ps")
+                    for hf in range(2):
+                        for s_ in range(2):
+                            for g in range(HG * hf, HG * (hf + 1)):
+                                nc.tensor.matmul_mx(
+                                    out=first[s_][:],
+                                    lhsT=xh[hf][:, g - HG * hf, 256 * s_:256 * (s_ + 1)].bitcast(FP4X4),
+                                    lhsT_scale=xp[0][:, g, 128 * s_:128 * (s_ + 1)],
+                                    rhs=wkh[hf][:, g - HG * hf, :].bitcast(FP4X4),
+                                    rhs_scale=wp[KK][:, g, :],
+                                    start=(g == 0), stop=(g == G - 1),
+                                )
                 for n_, wd in enumerate(widths):
+                    if step < 2:
+                        ps = first[step]
+                        banks.append(ps)
+                        continue
                     ps = psum.tile([P, 512], F32, name="ps")
                     banks.append(ps)
                     for g in range(G):
+                        if kind == KK:
+                            codes = wkh[g // HG][:, g % HG, :]
+                        else:
+                            codes = wc[kind][:, g, 2 * wd * n_:2 * wd * (n_ + 1)]
+                        if cc == 0:
+                            x_codes = xh[g // HG][:, g % HG, 256 * tc_:256 * (tc_ + 1)]
+                        else:
+                            x_codes = xc[cc][:, g, 256 * tc_:256 * (tc_ + 1)]
                         nc.tensor.matmul_mx(
                             out=ps[:, 0:wd],
-                            lhsT=xc[cc][:, g, 256 * tc_:256 * (tc_ + 1)].bitcast(FP4X4),
+                            lhsT=x_codes.bitcast(FP4X4),
                             lhsT_scale=xp[c][:, g, 128 * tl:128 * (tl + 1)],
-                            rhs=wc[kind][:, g, 2 * wd * n_:2 * wd * (n_ + 1)].bitcast(FP4X4),
+                            rhs=codes.bitcast(FP4X4),
                             rhs_scale=wp[kind][:, g, wd * n_:wd * (n_ + 1)],
                             start=(g == 0), stop=(g == G - 1),
                         )

@@ -78,8 +78,8 @@ def tile_gemma3mhattention_pa_kernel(
         for c, (ta, tb) in enumerate(CHUNKS):
             xp.append(keep.tile([P, G, 128 * (tb - ta)], U8, name="xp%d" % c, align_bytes=256))
 
-        def load_planes(planes, scales):
-            for q in range(4):
+        def load_planes(planes, scales, quadrants=(0, 1, 2, 3)):
+            for q in quadrants:
                 nc.sync.dma_start(
                     out=planes[32 * q:32 * q + 4, :, :].bitcast(I32),
                     in_=scales[:, 4 * q:4 * q + 4, :].rearrange("g r n -> r g n").bitcast(I32),
@@ -117,9 +117,9 @@ def tile_gemma3mhattention_pa_kernel(
 
         load_codes(xh[0], x_words[0:HG, :, 0:512])
         load_codes(wkh[0], wk_words[0:HG])
-        nc.sync.dma_start(out=wrow[0:1, 0:DH], in_=k_norm_w.unsqueeze(0))
         load_planes(xp[0], x_scales[:, :, 0:128 * CHUNKS[0][1]])
-        load_planes(wp[KK], w_src[KK][1])
+        load_planes(wp[KK], w_src[KK][1], (0, 2, 1, 3))
+        nc.sync.dma_start(out=wrow[0:1, 0:DH], in_=k_norm_w.unsqueeze(0))
         nc.sync.dma_start(out=wrow[0:1, DH:2 * DH], in_=q_norm_w.unsqueeze(0))
         load_codes(xh[1], x_words[HG:G, :, 0:512])
         load_codes(wkh[1], wk_words[HG:G])
@@ -140,8 +140,6 @@ def tile_gemma3mhattention_pa_kernel(
             return wps[:, 0:DH]
 
         for w_ in range(N_WARM):
-            if w_ == N_WARM // 2:
-                wk_ps = spread(0)
             nc.tensor.matmul(out=warm[:], lhsT=zeros[:, 0:P], rhs=zeros[:], start=True, stop=True)
 
         dummy = keep.tile([P, 2], F32, name="dummy")
@@ -180,7 +178,6 @@ def tile_gemma3mhattention_pa_kernel(
             nc.scalar.activation(out=gs[:, HALF:DH], in_=w_bf[:, 0:HALF], func=AF.Copy, scale=s, bias=s)
             gains[kind] = (gn, gs)
 
-        make_gains(KK, wk_ps, 1.0)
         nc.scalar.activation(out=dummy[:, 1:2], in_=ones[:, 0:1], func=AF.Abs_reciprocal_sqrt, scale=1.0, bias=eps_t[:])
 
         tabs = {}
@@ -201,8 +198,6 @@ def tile_gemma3mhattention_pa_kernel(
                     in1=gg[:].rearrange("p (s c) -> p s c", s=2).unsqueeze(1).to_broadcast([P, n_i, 2, HALF]),
                     op=ALU.mult)
 
-        build_tables(nc.vector, KK, 0)
-        build_tables(nc.gpsimd, KK, 1)
         nc.gpsimd.memset(xp[2][:].bitcast(F32), 0.0)
 
         def chunk_of(chunks, t):
@@ -332,6 +327,8 @@ def tile_gemma3mhattention_pa_kernel(
                     for s_ in range(2):
                         first[s_] = psum.tile([P, 512], F32, name="ps")
                     for hf in range(2):
+                        if hf == 1:
+                            wk_ps = spread(0)
                         for s_ in range(2):
                             for g in range(HG * hf, HG * (hf + 1)):
                                 nc.tensor.matmul_mx(
@@ -397,6 +394,10 @@ def tile_gemma3mhattention_pa_kernel(
                         batch[bi] = {"ss": ssb, "rs": rsb, "pp": ppb, "done": 0, "added": False, "members": []}
                     bt = batch[bi]
                     bt["members"].append((q, t, kind))
+                    if step == 0:
+                        make_gains(KK, wk_ps, 1.0)
+                        build_tables(nc.vector, KK, 0)
+                        build_tables(nc.gpsimd, KK, 1)
                     for h in range(4):
                         junk = small.tile([P, DH], F32, name="junk", align_bytes=256)
                         nc.scalar.activation(out=junk[:], in_=ps[:, DH * h:DH * (h + 1)], func=AF.Square,

@@ -30,6 +30,7 @@ LAGB = 7
 N_PLAIN = 6
 N_SINGLE = 24
 N_NOW = 3
+N_FIRST = 4
 V_FRONT = 0
 V_BACK = 6
 N_WARM = 8
@@ -402,16 +403,16 @@ def tile_gemma3mhattention_pa_kernel(
                         junk = small.tile([P, DH], F32, name="junk", align_bytes=256)
                         nc.scalar.activation(out=junk[:], in_=ps[:, DH * h:DH * (h + 1)], func=AF.Square,
                                              accum_out=bt["ss"][:, 4 * j + h:4 * j + h + 1])
-                    if step == 0:
-                        make_gains(Q0, wq_ps, QS)
-                        build_tables(nc.vector, Q0, 0)
-                        build_tables(nc.gpsimd, Q0, 1)
                     rsqrt_and_products(step)
                     if is_wide(q):
                         products(q, t, kind, ps)
                     state["pend"] = (q, t, kind, ps)
-                    if q >= n_qk - N_NOW:
+                    if q >= n_qk - N_NOW or q < N_FIRST:
                         rsqrt_and_products(step)
+                    if step == 0:
+                        make_gains(Q0, wq_ps, QS)
+                        build_tables(nc.gpsimd, Q0, 0)
+                        build_tables(nc.gpsimd, Q0, 1)
             else:
                 rsqrt_and_products(step)
             for bi in due.get(step, []):

@@ -30,7 +30,7 @@ LAGB = 7
 N_PLAIN = 6
 N_SINGLE = 24
 N_NOW = 3
-N_FIRST = 4
+N_FIRST = 96
 V_FRONT = 0
 V_BACK = 6
 N_WARM = 8

from contextlib import ExitStack
import math

import concourse.mybir as mybir

F32 = mybir.dt.float32
BF16 = mybir.dt.bfloat16
I32 = mybir.dt.int32
U8 = mybir.dt.uint8
FP4X4 = mybir.dt.float4_e2m1fn_x4
ALU = mybir.AluOpType
AF = mybir.ActivationFunctionType

B, T, E, H, HKV, DH = 4, 1024, 2048, 8, 4, 128
THETA = 10000.0
EPS = 1e-6
P = 128
G = E // 512
NT = B * T // P
TPB = T // P
HALF = DH // 2
QS = DH ** -0.5

FLOPS = 2 * B * T * E * (H + 2 * HKV) * DH

Q0, Q1, KK, VV = 0, 1, 2, 3
N_WIDE = 0
NB = 3
LAGB = 7
N_PLAIN = 6
N_SINGLE = 24
N_NOW = 3
N_FIRST = 96
V_FRONT = 0
V_BACK = 6
N_WARM = 8
CHUNKS = ((0, 4), (4, 8), (8, 16), (16, 24), (24, 32))
CODE_CHUNKS = ((0, 2), (2, 4)) + CHUNKS[1:]
HG = G // 2


def tile_gemma3mhattention_pa_kernel(
    tc, x_words, x_scales, wq_words, wq_scales, wk_words, wk_scales, wv_words, wv_scales,
    q_norm_w, k_norm_w, out_0, out_1, out_2,
):
    nc = tc.nc
    with ExitStack() as ctx:
        keep = ctx.enter_context(tc.tile_pool(name="keep", bufs=1))
        small = ctx.enter_context(tc.tile_pool(name="small", bufs=6))
        work = ctx.enter_context(tc.tile_pool(name="work", bufs=4))
        prod = ctx.enter_context(tc.tile_pool(name="prod", bufs=3))
        psum = ctx.enter_context(tc.psum_pool(name="psum", bufs=8))
        ctx.enter_context(tc.manual_schedule())

        w_src = {
            Q0: (wq_words[:, :, 0:1024], wq_scales[:, :, 0:512]),
            Q1: (wq_words[:, :, 1024:2048], wq_scales[:, :, 512:1024]),
            KK: (wk_words, wk_scales),
            VV: (wv_words, wv_scales),
        }
        wc = {}
        wp = {}
        for kind in (VV, KK, Q0, Q1):
            if kind != KK:
                wc[kind] = keep.tile([P, G, 1024], U8, name="wc%d" % kind, align_bytes=256)
            wp[kind] = keep.tile([P, G, 512], U8, name="wp%d" % kind, align_bytes=256)
        xh = []
        wkh = []
        for hf in range(2):
            xh.append(keep.tile([P, HG, 512], U8, name="xh%d" % hf, align_bytes=256))
            wkh.append(keep.tile([P, HG, 1024], U8, name="wkh%d" % hf, align_bytes=256))
        xc = []
        xp = []
        for c, (ta, tb) in enumerate(CODE_CHUNKS):
            if c == 0:
                xc.append(None)
            else:
                xc.append(keep.tile([P, G, 256 * (tb - ta)], U8, name="xc%d" % c, align_bytes=256))
        for c, (ta, tb) in enumerate(CHUNKS):
            xp.append(keep.tile([P, G, 128 * (tb - ta)], U8, name="xp%d" % c, align_bytes=256))

        def load_planes(planes, scales, quadrants=(0, 1, 2, 3)):
            for q in quadrants:
                nc.sync.dma_start(
                    out=planes[32 * q:32 * q + 4, :, :].bitcast(I32),
                    in_=scales[:, 4 * q:4 * q + 4, :].rearrange("g r n -> r g n").bitcast(I32),
                )

        def load_codes(codes, words):
            nc.sync.dma_start(out=codes[:].bitcast(I32), in_=words.rearrange("g p n -> p g n").bitcast(I32))

        def load_x_codes(c):
            ta, tb = CODE_CHUNKS[c]
            load_codes(xc[c], x_words[:, :, 256 * ta:256 * tb])

        def load_x(c):
            ta, tb = CHUNKS[c]
            load_planes(xp[c], x_scales[:, :, 128 * ta:128 * tb])
            load_x_codes(c + 1)

        def load_w(kind):
            load_planes(wp[kind], w_src[kind][1])
            load_codes(wc[kind], w_src[kind][0])

        pos = keep.tile([P, TPB], F32, name="pos")
        wrow = keep.tile([P, 2 * DH], BF16, name="wrow")
        ones_bf = keep.tile([P, P], BF16, name="ones_bf")
        nc.vector.memset(wrow[:], 0.0)
        nc.gpsimd.memset(xp[0][:].bitcast(F32), 0.0)
        nc.gpsimd.memset(wp[KK][:].bitcast(F32), 0.0)
        nc.gpsimd.iota(pos[:], pattern=[[P, TPB]], base=0, channel_multiplier=1,
                       allow_small_or_imprecise_dtypes=True)
        for t_ in (wp[Q0], wp[VV], wp[Q1], xp[1]):
            nc.gpsimd.memset(t_[:].bitcast(F32), 0.0)

        ones = keep.tile([P, 8], F32, name="ones")
        nc.vector.memset(ones[:], 1.0)

        load_codes(xh[0], x_words[0:HG, :, 0:512])
        load_codes(wkh[0], wk_words[0:HG])
        load_planes(xp[0], x_scales[:, :, 0:128 * CHUNKS[0][1]])
        load_planes(wp[KK], w_src[KK][1], (0, 2, 1, 3))
        nc.sync.dma_start(out=wrow[0:1, 0:DH], in_=k_norm_w.unsqueeze(0))
        nc.sync.dma_start(out=wrow[0:1, DH:2 * DH], in_=q_norm_w.unsqueeze(0))
        load_codes(xh[1], x_words[HG:G, :, 0:512])
        load_codes(wkh[1], wk_words[HG:G])
        load_x_codes(1)
        load_w(Q0)
        load_w(VV)
        load_w(Q1)
        load_x(1)

        zeros = keep.tile([P, 512], BF16, name="zeros")
        nc.vector.memset(zeros[:], 0.0)
        nc.vector.memset(ones_bf[:], 1.0)
        warm = psum.tile([P, 512], F32, name="ps")

        def spread(c0):
            wps = psum.tile([P, 512], F32, name="ps")
            nc.tensor.matmul(out=wps[:, 0:DH], lhsT=ones_bf[:], rhs=wrow[:, c0:c0 + DH], start=True, stop=True)
            return wps[:, 0:DH]

        for w_ in range(N_WARM):
            nc.tensor.matmul(out=warm[:], lhsT=zeros[:, 0:P], rhs=zeros[:], start=True, stop=True)

        dummy = keep.tile([P, 2], F32, name="dummy")
        nc.scalar.activation(out=dummy[:, 0:1], in_=ones[:, 0:1], func=AF.Sin, scale=1.0)
        fa = keep.tile([P, 8], F32, name="fa")
        fb = keep.tile([P, 8], F32, name="fb")
        for a in range(8):
            nc.scalar.activation(out=fa[:, a:a + 1], in_=ones[:, a:a + 1], func=AF.Copy,
                                 scale=THETA ** (-(8.0 * a) / HALF) / (2.0 * math.pi))
            nc.vector.tensor_scalar(out=fb[:, a:a + 1], in0=ones[:, a:a + 1],
                                    scalar1=THETA ** (-(1.0 * a) / HALF), scalar2=None, op0=ALU.mult)
        eps_t = keep.tile([P, 1], F32, name="eps_t")
        nc.scalar.activation(out=eps_t[:], in_=ones[:, 0:1], func=AF.Copy, scale=EPS)
        freq = keep.tile([P, HALF], F32, name="freq")
        nc.vector.tensor_tensor(out=freq[:].rearrange("p (a b) -> p a b", a=8),
                                in0=fa[:].unsqueeze(2).to_broadcast([P, 8, 8]),
                                in1=fb[:].unsqueeze(1).to_broadcast([P, 8, 8]), op=ALU.mult)
        ph = keep.tile([P, 2, TPB, HALF], F32, name="ph")
        nc.vector.tensor_tensor(out=ph[:, 0], in0=pos[:].unsqueeze(2).to_broadcast([P, TPB, HALF]),
                                in1=freq[:].unsqueeze(1).to_broadcast([P, TPB, HALF]), op=ALU.mult)
        nc.scalar.activation(out=ph[:, 1], in_=ph[:, 0], func=AF.Copy, scale=1.0, bias=0.25)
        ni = keep.tile([P, 2, TPB, HALF], I32, name="ni")
        fr = keep.tile([P, 2, TPB, HALF], F32, name="fr")
        sc = keep.tile([P, 2, TPB, HALF], F32, name="sc")
        gains = {}
        for k in range(2):
            nc.vector.tensor_copy(out=ni[:, k], in_=ph[:, k])
            nc.vector.tensor_tensor(out=fr[:, k], in0=ph[:, k], in1=ni[:, k], op=ALU.subtract)
            nc.scalar.activation(out=sc[:, k], in_=fr[:, k], func=AF.Sin, scale=2.0 * math.pi)

        def make_gains(kind, w_bf, s):
            gn = keep.tile([P, DH], F32, name="gn%d" % kind)
            gs = keep.tile([P, DH], F32, name="gs%d" % kind)
            nc.scalar.activation(out=gn[:], in_=w_bf, func=AF.Copy, scale=s, bias=s)
            nc.scalar.activation(out=gs[:, 0:HALF], in_=w_bf[:, HALF:DH], func=AF.Copy, scale=-s, bias=-s)
            nc.scalar.activation(out=gs[:, HALF:DH], in_=w_bf[:, 0:HALF], func=AF.Copy, scale=s, bias=s)
            gains[kind] = (gn, gs)

        nc.scalar.activation(out=dummy[:, 1:2], in_=ones[:, 0:1], func=AF.Abs_reciprocal_sqrt, scale=1.0, bias=eps_t[:])

        tabs = {}
        for kind in (KK, Q0):
            for half in range(2):
                tab_ = keep.tile([P, TPB // 2, 2 * DH], F32, name="tab%d%d" % (kind, half), align_bytes=256)
                tabs[(kind, half)] = tab_
                tabs[(Q1 if kind == Q0 else kind, half)] = tab_

        def build_tables(eng, kind, half):
            gn, gs = gains[kind]
            blocks = tabs[(kind, half)][:].rearrange("p i (b c) -> p i b c", b=4)
            n_i = TPB // 2
            for sel, k, gg in ((slice(1, 3), 0, gs), (slice(0, 4, 3), 1, gn)):
                eng.tensor_tensor(
                    out=blocks[:, :, sel, :],
                    in0=sc[:, k, n_i * half:n_i * (half + 1), :].unsqueeze(2).to_broadcast([P, n_i, 2, HALF]),
                    in1=gg[:].rearrange("p (s c) -> p s c", s=2).unsqueeze(1).to_broadcast([P, n_i, 2, HALF]),
                    op=ALU.mult)

        nc.gpsimd.memset(xp[2][:].bitcast(F32), 0.0)

        def chunk_of(chunks, t):
            for c, (ta, tb) in enumerate(chunks):
                if ta <= t < tb:
                    return c, t - ta
            raise ValueError("token tile out of range")

        def dest(t, kind):
            b, i = divmod(t, TPB)
            rows = slice(P * i, P * (i + 1))
            if kind == Q0:
                d = out_0[b, 0:4, rows, :]
            elif kind == Q1:
                d = out_0[b, 4:8, rows, :]
            elif kind == KK:
                d = out_1[b, :, rows, :]
            else:
                d = out_2[b, :, rows, :]
            return d.rearrange("h p c -> p h c")

        qk = []
        for kind in (KK, Q0, Q1):
            for t in range(4):
                qk.append((t, kind))
        for t in range(4, NT):
            for kind in (Q0, Q1, KK):
                qk.append((t, kind))
        n_mid = NT - V_FRONT - V_BACK
        seq = []
        for t in range(V_FRONT):
            seq.append((t, VV))
        for j in range(NT):
            seq.extend(qk[3 * j:3 * j + 3])
            if (j + 1) * n_mid // NT > j * n_mid // NT and j < NT - 1:
                seq.append((len(seq) - 3 * (j + 1), VV))
        for t in range(len(seq) - 3 * NT, NT):
            seq.append((t, VV))
        n_qk = 3 * NT
        sizes = [NB] * ((n_qk - N_SINGLE) // NB) + [1] * N_SINGLE
        place = []
        for bi, size in enumerate(sizes):
            for j in range(size):
                place.append((bi, j))
        x_after = {10: 2, 28: 3, 60: 4}
        zero_after = {2: 3, 5: 4}
        batch = {}
        due = {}
        state = {"q": 0, "pend": None}
        first = {}

        def is_wide(q):
            return (q + 1) * N_WIDE // n_qk > q * N_WIDE // n_qk and q < n_qk - N_PLAIN

        def products(q, t, kind, ps):
            bi, j = place[q]
            bt = batch[bi]
            i = t % TPB
            base = 1024 * j
            tab = tabs[(kind, i // (TPB // 2))][:, i % (TPB // 2), :].rearrange("p (s c) -> p s c", s=2)
            if is_wide(q):
                nc.vector.tensor_tensor(out=bt["pp"][:, base:base + 1024].rearrange("p (h s c) -> p h s c", h=4, s=2),
                                        in0=ps[:].rearrange("p (h c) -> p h c", h=4).unsqueeze(2).to_broadcast([P, 4, 2, DH]),
                                        in1=tab.unsqueeze(1).to_broadcast([P, 4, 2, DH]), op=ALU.mult)
            else:
                for h in range(4):
                    r = bt["rs"][:, 4 * j + h:4 * j + h + 1]
                    nc.vector.scalar_tensor_tensor(
                        out=bt["pp"][:, base + 2 * DH * h:base + 2 * DH * (h + 1)].rearrange("p (s c) -> p s c", s=2),
                        in0=ps[:, DH * h:DH * (h + 1)].unsqueeze(1).to_broadcast([P, 2, DH]), scalar=r,
                        in1=tab, op0=ALU.mult, op1=ALU.mult)
            bt["done"] += 1

        def maybe_add(bi, step):
            bt = batch[bi]
            if bt["done"] < sizes[bi] or bt["added"]:
                return
            w = 512 * sizes[bi]
            if sizes[bi] > 1:
                ob = work.tile([P, 512 * NB], F32, name="ob", bufs=6, align_bytes=256)
            else:
                ob = work.tile([P, 512], F32, name="ob1", bufs=8, align_bytes=256)
            ppv = bt["pp"][:, 0:2 * w].rearrange("p (m k c) -> p m k c", k=2, c=HALF)
            nc.gpsimd.tensor_tensor(out=ob[:, 0:w].rearrange("p (m c) -> p m c", c=HALF),
                                    in0=ppv[:, :, 0, :], in1=ppv[:, :, 1, :], op=ALU.add)
            bt["ob"] = ob
            bt["added"] = True
            if bi in zero_after:
                nc.gpsimd.memset(xp[zero_after[bi]][:].bitcast(F32), 0.0)
            lag = LAGB if sizes[bi] > 1 else 4
            due.setdefault(step + lag, []).append(bi)

        def finish(bi):
            bt = batch[bi]
            for j, (q, t, kind) in enumerate(bt["members"]):
                base = 512 * j
                if is_wide(q):
                    for h in range(4):
                        cols = slice(base + DH * h, base + DH * (h + 1))
                        nc.scalar.activation(out=bt["ob"][:, cols], in_=bt["ob"][:, cols], func=AF.Copy,
                                             scale=bt["rs"][:, 4 * j + h:4 * j + h + 1])
                nc.sync.dma_start(out=dest(t, kind),
                                  in_=bt["ob"][:, base:base + 512].rearrange("p (h c) -> p h c", h=4))

        def rsqrt_and_products(step):
            if state["pend"] is None:
                return
            q, t, kind, ps = state["pend"]
            state["pend"] = None
            bi, j = place[q]
            bt = batch[bi]
            nc.scalar.activation(out=bt["rs"][:, 4 * j:4 * j + 4], in_=bt["ss"][:, 4 * j:4 * j + 4],
                                 func=AF.Abs_reciprocal_sqrt, scale=1.0 / DH, bias=eps_t[:])
            if not is_wide(q):
                products(q, t, kind, ps)
            maybe_add(bi, step)

        last = len(seq) + LAGB + 2
        for step in range(last):
            if step < len(seq):
                t, kind = seq[step]
                c, tl = chunk_of(CHUNKS, t)
                cc, tc_ = chunk_of(CODE_CHUNKS, t)
                widths = [512] if step < len(seq) - 1 else [DH] * 4
                banks = []
                if step == 0:
                    for s_ in range(2):
                        first[s_] = psum.tile([P, 512], F32, name="ps")
                    for hf in range(2):
                        if hf == 1:
                            wk_ps = spread(0)
                        for s_ in range(2):
                            for g in range(HG * hf, HG * (hf + 1)):
                                nc.tensor.matmul_mx(
                                    out=first[s_][:],
                                    lhsT=xh[hf][:, g - HG * hf, 256 * s_:256 * (s_ + 1)].bitcast(FP4X4),
                                    lhsT_scale=xp[0][:, g, 128 * s_:128 * (s_ + 1)],
                                    rhs=wkh[hf][:, g - HG * hf, :].bitcast(FP4X4),
                                    rhs_scale=wp[KK][:, g, :],
                                    start=(g == 0), stop=(g == G - 1),
                                )
                for n_, wd in enumerate(widths):
                    if step < 2:
                        ps = first[step]
                        banks.append(ps)
                        continue
                    ps = psum.tile([P, 512], F32, name="ps")
                    banks.append(ps)
                    for g in range(G):
                        if kind == KK:
                            codes = wkh[g // HG][:, g % HG, :]
                        else:
                            codes = wc[kind][:, g, 2 * wd * n_:2 * wd * (n_ + 1)]
                        if cc == 0:
                            x_codes = xh[g // HG][:, g % HG, 256 * tc_:256 * (tc_ + 1)]
                        else:
                            x_codes = xc[cc][:, g, 256 * tc_:256 * (tc_ + 1)]
                        nc.tensor.matmul_mx(
                            out=ps[:, 0:wd],
                            lhsT=x_codes.bitcast(FP4X4),
                            lhsT_scale=xp[c][:, g, 128 * tl:128 * (tl + 1)],
                            rhs=codes.bitcast(FP4X4),
                            rhs_scale=wp[kind][:, g, wd * n_:wd * (n_ + 1)],
                            start=(g == 0), stop=(g == G - 1),
                        )
                if step == 0:
                    wq_ps = spread(DH)
                if len(banks) > 1:
                    vo = work.tile([P, 512], F32, name="vo", align_bytes=256)
                    for h, ps in enumerate(banks):
                        cols = slice(DH * h, DH * (h + 1))
                        if h % 2 == 0:
                            nc.scalar.copy(out=vo[:, cols], in_=ps[:, 0:DH])
                        else:
                            nc.vector.tensor_copy(out=vo[:, cols], in_=ps[:, 0:DH])
                        nc.sync.dma_start(out=dest(t, kind)[:, h, :], in_=vo[:, cols])
                    rsqrt_and_products(step)
                elif kind == VV:
                    vo = work.tile([P, 512], F32, name="vo", align_bytes=256)
                    nc.scalar.copy(out=vo[:], in_=ps[:])
                    nc.sync.dma_start(out=dest(t, kind), in_=vo[:].rearrange("p (h c) -> p h c", h=4))
                    rsqrt_and_products(step)
                else:
                    q = state["q"]
                    state["q"] = q + 1
                    bi, j = place[q]
                    if j == 0:
                        ssb = small.tile([P, 4 * NB], F32, name="ssb")
                        rsb = small.tile([P, 4 * NB], F32, name="rsb")
                        if sizes[bi] > 1:
                            ppb = prod.tile([P, 1024 * NB], F32, name="ppb", align_bytes=256)
                        else:
                            ppb = prod.tile([P, 1024], F32, name="pp1", bufs=5, align_bytes=256)
                        batch[bi] = {"ss": ssb, "rs": rsb, "pp": ppb, "done": 0, "added": False, "members": []}
                    bt = batch[bi]
                    bt["members"].append((q, t, kind))
                    if step == 0:
                        make_gains(KK, wk_ps, 1.0)
                        build_tables(nc.vector, KK, 0)
                        build_tables(nc.gpsimd, KK, 1)
                    for h in range(4):
                        junk = small.tile([P, DH], F32, name="junk", align_bytes=256)
                        nc.scalar.activation(out=junk[:], in_=ps[:, DH * h:DH * (h + 1)], func=AF.Square,
                                             accum_out=bt["ss"][:, 4 * j + h:4 * j + h + 1])
                    rsqrt_and_products(step)
                    if is_wide(q):
                        products(q, t, kind, ps)
                    state["pend"] = (q, t, kind, ps)
                    if q >= n_qk - N_NOW or q < N_FIRST:
                        rsqrt_and_products(step)
                    if step == 0:
                        make_gains(Q0, wq_ps, QS)
                        build_tables(nc.gpsimd, Q0, 0)
                        build_tables(nc.gpsimd, Q0, 1)
            else:
                rsqrt_and_products(step)
            for bi in due.get(step, []):
                finish(bi)
            if step in x_after:
                load_x(x_after[step])
